import numpy as np
import ml_dtypes


def mxq(x, axis, fmt="e4m3"):
    dtype, down = {"e4m3": (ml_dtypes.float8_e4m3fn, 7), "e5m2": (ml_dtypes.float8_e5m2, 14)}[fmt]
    v = np.moveaxis(np.asarray(x, np.float32).astype(ml_dtypes.bfloat16).astype(np.float64), axis, -1)
    blocks = v.reshape(v.shape[:-1] + (-1, 32))
    amax = np.abs(blocks).max(-1, keepdims=True)
    byte = np.maximum(np.where(amax > 0, np.frexp(amax)[1] - 1 + 127, 0) - down, 1)
    scale = np.exp2(byte - 127.0)
    codes = (blocks / scale).astype(np.float32).astype(dtype).astype(np.float64)
    return np.moveaxis((codes * scale).reshape(v.shape), -1, axis)


WIDE = False


def mx_kscale(k):
    if not WIDE:
        return np.ones(k)
    levels = np.array([20, -20, 10, -10, 0])
    a = np.random.permutation(np.resize(levels, k // 512 * 4)).reshape(k // 512, 4)
    idx = np.arange(k)
    return np.exp2(a[idx // 512, idx % 128 // 32])


BF16 = ml_dtypes.bfloat16


def bf(x):
    return np.asarray(x, np.float32).astype(BF16)


def f64(x):
    return np.asarray(x).astype(np.float64)


N, M, D, B = 256, 512, 4, 1024
MD = M * D


def sigmoid(v):
    return 1.0 / (1.0 + np.exp(-v))


def diag_mask():
    return np.broadcast_to((1.0 - np.eye(M))[:, :, None], (M, M, D)).reshape(M, MD)


def tri_mask():
    return f64(np.arange(D)[:, None] < np.arange(D)[None, :])


def big_diag(w):
    w3 = w.reshape(M, M, D).copy()
    i = np.arange(M)
    w3[i, i, :] = np.random.standard_normal((M, D)) * 0.5
    return w3.reshape(M, MD)


def setup_inputs():
    r = np.random.standard_normal
    s = mx_kscale(B)[:, None]
    ca, cb = 0.7 / np.sqrt(M), 0.7 / np.sqrt(N)
    x_t = bf(r((B, N)))
    m0 = bf(r((B, M)))
    a_t = bf(r((B, MD)))
    A_fg = bf(r((M, MD)) * ca)
    A_in = bf(r((M, MD)) * ca)
    A_th = bf(big_diag(r((M, MD)) * ca))
    A_pt_blk = bf(r((M, D, D)) * 0.4)
    B_fg = bf(r((N, MD)) * cb)
    B_in = bf(r((N, MD)) * cb)
    B_th = bf(r((N, MD)) * cb)
    b_fg = bf(r((1, MD)) * 0.3)
    b_in = bf(r((1, MD)) * 0.3)
    b_th = bf(r((1, MD)) * 0.3)
    g = bf(r((B, MD)) * np.exp2(np.random.randint(-12, 1, (B, 1))) / s)
    G = sigmoid(f64(m0) @ f64(A_fg) + f64(x_t) @ f64(B_fg) + f64(b_fg))
    return {"x_t": x_t, "m_t": bf(f64(m0) * s), "a_t": a_t,
            "A_fg": A_fg, "A_in": A_in, "A_th": A_th, "A_pt_blk": A_pt_blk,
            "B_fg": B_fg, "B_in": B_in, "B_th": B_th,
            "b_fg": b_fg, "b_in": b_in, "b_th": b_th,
            "G_fg": np.asarray(G, np.float32), "grad_out": g}


def reference(x_t, m_t, a_t, A_fg, A_in, A_th, A_pt_blk, B_fg, B_in, B_th, b_fg, b_in, b_th, G_fg, grad_out):
    G = f64(G_fg)
    dz = f64(grad_out) * f64(a_t) * (G * (1.0 - G))
    return mxq(f64(m_t), 0, "e4m3").T @ mxq(dz, 0, "e5m2")

@@ -1,0 +1,139 @@
+import concourse.mybir as mybir
+
+F32 = mybir.dt.float32
+BF16 = mybir.dt.bfloat16
+U32 = mybir.dt.uint32
+U8 = mybir.dt.uint8
+E4M3_X4 = mybir.dt.float8_e4m3fn_x4
+E5M2_X4 = mybir.dt.float8_e5m2_x4
+MULT = mybir.AluOpType.mult
+SUBTRACT = mybir.AluOpType.subtract
+
+P = 128
+PACK = 4
+K_PASS = P * PACK
+TOKENS = 1024
+M = 512
+MD = 2048
+PASSES = TOKENS // K_PASS
+M_TILE = P
+M_TILES = M // M_TILE
+N_TILE = 512
+CHUNKS = MD // N_TILE
+RUN = 4
+
+FLOPS = 2 * TOKENS * M * MD
+BYTES = TOKENS * M * 2 + TOKENS * MD * (2 + 2 + 4) + M * MD * 4
+
+
+def rows_apart(tile_ap):
+    return tile_ap.rearrange("p j (q i) -> p q j i", i=RUN)
+
+
+def rows_together(tile_ap):
+    return tile_ap.rearrange("p (q i) j -> p q j i", i=RUN)
+
+
+def tile_edrncell_pa_v_kernel(
+    tc, x_t, m_t, a_t, A_fg, A_in, A_th, A_pt_blk, B_fg, B_in, B_th, b_fg, b_in, b_th, G_fg, grad_out, out
+):
+    nc = tc.nc
+    gate_rows = G_fg.rearrange("(c p j) w -> c p j w", p=P, j=PACK)
+    grad_rows = grad_out.rearrange("(c p j) w -> c p j w", p=P, j=PACK)
+    act_rows = a_t.rearrange("(c p j) w -> c p j w", p=P, j=PACK)
+
+    with (
+        tc.tile_pool(name="inputs", bufs=CHUNKS * PASSES) as inputs,
+        tc.tile_pool(name="keep", bufs=1) as keep,
+        tc.tile_pool(name="stage", bufs=4) as stage,
+        tc.psum_pool(name="psum", bufs=2) as psum,
+    ):
+        gate, grad, act, dz = {}, {}, {}, {}
+
+        def load_chunk(n):
+            cols = slice(n * N_TILE, (n + 1) * N_TILE)
+            for c in range(PASSES):
+                gate_tile = inputs.tile([P, PACK, N_TILE], F32)
+                nc.sync.dma_start(out=gate_tile[:], in_=gate_rows[c, :, :, cols])
+                gate[n, c] = gate_tile
+            for c in range(PASSES):
+                grad_tile = inputs.tile([P, PACK, N_TILE], BF16)
+                nc.sync.dma_start(out=grad_tile[:], in_=grad_rows[c, :, :, cols])
+                grad[n, c] = grad_tile
+            for c in range(PASSES):
+                act_tile = inputs.tile([P, PACK, N_TILE], BF16)
+                nc.sync.dma_start(out=act_tile[:], in_=act_rows[c, :, :, cols])
+                act[n, c] = act_tile
+
+        def products(n):
+            for c in range(PASSES):
+                g = gate[n, c]
+                nc.vector.scalar_tensor_tensor(
+                    out=g[:], in0=g[:], scalar=1.0, in1=g[:], op0=SUBTRACT, op1=MULT
+                )
+            for c in range(PASSES):
+                g = gate[n, c]
+                nc.vector.scalar_tensor_tensor(
+                    out=g[:], in0=g[:], scalar=-1.0, in1=grad[n, c][:], op0=MULT, op1=MULT
+                )
+            for c in range(PASSES):
+                dz_tile = stage.tile([P, N_TILE, PACK], BF16, align_bytes=64)
+                nc.vector.tensor_tensor(
+                    out=rows_together(dz_tile[:]),
+                    in0=rows_apart(gate[n, c][:]),
+                    in1=rows_apart(act[n, c][:]),
+                    op=MULT,
+                )
+                dz[n, c] = dz_tile
+
+        def quantise_and_multiply(n):
+            cols = slice(n * N_TILE, (n + 1) * N_TILE)
+            acc = [psum.tile([M_TILE, N_TILE], F32, name="acc%d" % t) for t in range(M_TILES)]
+            for c in range(PASSES):
+                nc.vector.quantize_mx(
+                    out=dz_codes[:, c, cols].bitcast(E5M2_X4),
+                    scales=dz_scales[:, c, cols],
+                    in_=dz[n, c][:].rearrange("p w j -> p (w j)"),
+                )
+                for t in range(M_TILES):
+                    m_cols = slice(t * M_TILE, (t + 1) * M_TILE)
+                    nc.tensor.matmul_mx(
+                        out=acc[t][:],
+                        lhsT=m_codes[:, c, m_cols].bitcast(E4M3_X4),
+                        lhsT_scale=m_scales[:, c, m_cols],
+                        rhs=dz_codes[:, c, cols].bitcast(E5M2_X4),
+                        rhs_scale=dz_scales[:, c, cols],
+                        start=(c == 0),
+                        stop=(c == PASSES - 1),
+                    )
+            for t in range(M_TILES):
+                result = stage.tile([M_TILE, N_TILE], F32)
+                nc.scalar.copy(out=result[:], in_=acc[t][:])
+                nc.sync.dma_start(out=out[t * M_TILE : (t + 1) * M_TILE, cols], in_=result[:])
+
+        load_chunk(0)
+        m_raw = keep.tile([P, PASSES, PACK, M], BF16)
+        nc.sync.dma_start(out=m_raw[:], in_=m_t.rearrange("(c p j) i -> p c j i", p=P, j=PACK))
+        for n in range(1, CHUNKS):
+            load_chunk(n)
+
+        m_codes = keep.tile([P, PASSES, M], U32, align_bytes=64)
+        m_scales = keep.tile([P, PASSES, M], U8, align_bytes=64)
+        dz_codes = keep.tile([P, PASSES, MD], U32, align_bytes=64)
+        dz_scales = keep.tile([P, PASSES, MD], U8, align_bytes=64)
+
+        products(0)
+
+        m_grouped = keep.tile([P, PASSES, M, PACK], BF16, align_bytes=64)
+        for c in range(PASSES):
+            nc.scalar.copy(out=rows_together(m_grouped[:, c]), in_=rows_apart(m_raw[:, c]))
+        nc.vector.quantize_mx(
+            out=m_codes[:].rearrange("p c i -> p (c i)").bitcast(E4M3_X4),
+            scales=m_scales[:].rearrange("p c i -> p (c i)"),
+            in_=m_grouped[:].rearrange("p c i j -> p (c i j)"),
+        )
+
+        quantise_and_multiply(0)
+        for n in range(1, CHUNKS):
+            products(n)
+            quantise_and_multiply(n)

@@ -47,6 +47,7 @@ def tile_edrncell_pa_v_kernel(
         tc.tile_pool(name="keep", bufs=1) as keep,
         tc.tile_pool(name="stage", bufs=4) as stage,
         tc.psum_pool(name="psum", bufs=2) as psum,
+        tc.manual_schedule(),
     ):
         gate, grad, act, dz = {}, {}, {}, {}
 
@@ -60,61 +61,64 @@ def tile_edrncell_pa_v_kernel(
                 grad_tile = inputs.tile([P, PACK, N_TILE], BF16)
                 nc.sync.dma_start(out=grad_tile[:], in_=grad_rows[c, :, :, cols])
                 grad[n, c] = grad_tile
+            if n == 0:
+                nc.sync.dma_start(out=m_raw[:], in_=m_t.rearrange("(c p j) i -> p c j i", p=P, j=PACK))
             for c in range(PASSES):
                 act_tile = inputs.tile([P, PACK, N_TILE], BF16)
                 nc.sync.dma_start(out=act_tile[:], in_=act_rows[c, :, :, cols])
                 act[n, c] = act_tile
 
-        def products(n):
-            for c in range(PASSES):
-                g = gate[n, c]
-                nc.vector.scalar_tensor_tensor(
-                    out=g[:], in0=g[:], scalar=1.0, in1=g[:], op0=SUBTRACT, op1=MULT
-                )
-            for c in range(PASSES):
-                g = gate[n, c]
-                nc.vector.scalar_tensor_tensor(
-                    out=g[:], in0=g[:], scalar=-1.0, in1=grad[n, c][:], op0=MULT, op1=MULT
-                )
-            for c in range(PASSES):
-                dz_tile = stage.tile([P, N_TILE, PACK], BF16, align_bytes=64)
-                nc.vector.tensor_tensor(
-                    out=rows_together(dz_tile[:]),
-                    in0=rows_apart(gate[n, c][:]),
-                    in1=rows_apart(act[n, c][:]),
-                    op=MULT,
-                )
-                dz[n, c] = dz_tile
+        def gate_derivative(n, c):
+            g = gate[n, c]
+            nc.vector.scalar_tensor_tensor(out=g[:], in0=g[:], scalar=1.0, in1=g[:], op0=SUBTRACT, op1=MULT)
 
-        def quantise_and_multiply(n):
+        def times_grad(n, c):
+            g = gate[n, c]
+            nc.vector.scalar_tensor_tensor(
+                out=g[:], in0=g[:], scalar=-1.0, in1=grad[n, c][:], op0=MULT, op1=MULT
+            )
+
+        def times_act(n, c):
+            dz_tile = stage.tile([P, N_TILE, PACK], BF16, align_bytes=64)
+            nc.vector.tensor_tensor(
+                out=rows_together(dz_tile[:]),
+                in0=rows_apart(gate[n, c][:]),
+                in1=rows_apart(act[n, c][:]),
+                op=MULT,
+            )
+            dz[n, c] = dz_tile
+
+        def quantise_and_multiply(n, c, acc):
             cols = slice(n * N_TILE, (n + 1) * N_TILE)
-            acc = [psum.tile([M_TILE, N_TILE], F32, name="acc%d" % t) for t in range(M_TILES)]
-            for c in range(PASSES):
-                nc.vector.quantize_mx(
-                    out=dz_codes[:, c, cols].bitcast(E5M2_X4),
-                    scales=dz_scales[:, c, cols],
-                    in_=dz[n, c][:].rearrange("p w j -> p (w j)"),
+            nc.vector.quantize_mx(
+                out=dz_codes[:, c, cols].bitcast(E5M2_X4),
+                scales=dz_scales[:, c, cols],
+                in_=dz[n, c][:].rearrange("p w j -> p (w j)"),
+            )
+            for t in range(M_TILES):
+                m_cols = slice(t * M_TILE, (t + 1) * M_TILE)
+                nc.tensor.matmul_mx(
+                    out=acc[t][:],
+                    lhsT=m_codes[:, c, m_cols].bitcast(E4M3_X4),
+                    lhsT_scale=m_scales[:, c, m_cols],
+                    rhs=dz_codes[:, c, cols].bitcast(E5M2_X4),
+                    rhs_scale=dz_scales[:, c, cols],
+                    start=(c == 0),
+                    stop=(c == PASSES - 1),
                 )
-                for t in range(M_TILES):
-                    m_cols = slice(t * M_TILE, (t + 1) * M_TILE)
-                    nc.tensor.matmul_mx(
-                        out=acc[t][:],
-                        lhsT=m_codes[:, c, m_cols].bitcast(E4M3_X4),
-                        lhsT_scale=m_scales[:, c, m_cols],
-                        rhs=dz_codes[:, c, cols].bitcast(E5M2_X4),
-                        rhs_scale=dz_scales[:, c, cols],
-                        start=(c == 0),
-                        stop=(c == PASSES - 1),
-                    )
+
+        def store(n, acc):
+            cols = slice(n * N_TILE, (n + 1) * N_TILE)
             for t in range(M_TILES):
                 result = stage.tile([M_TILE, N_TILE], F32)
-                nc.scalar.copy(out=result[:], in_=acc[t][:])
+                if n == CHUNKS - 1 and t % 2 == 1:
+                    nc.vector.tensor_copy(out=result[:], in_=acc[t][:])
+                else:
+                    nc.scalar.copy(out=result[:], in_=acc[t][:])
                 nc.sync.dma_start(out=out[t * M_TILE : (t + 1) * M_TILE, cols], in_=result[:])
 
-        load_chunk(0)
         m_raw = keep.tile([P, PASSES, PACK, M], BF16)
-        nc.sync.dma_start(out=m_raw[:], in_=m_t.rearrange("(c p j) i -> p c j i", p=P, j=PACK))
-        for n in range(1, CHUNKS):
+        for n in range(CHUNKS):
             load_chunk(n)
 
         m_codes = keep.tile([P, PASSES, M], U32, align_bytes=64)
@@ -122,18 +126,29 @@ def tile_edrncell_pa_v_kernel(
         dz_codes = keep.tile([P, PASSES, MD], U32, align_bytes=64)
         dz_scales = keep.tile([P, PASSES, MD], U8, align_bytes=64)
 
-        products(0)
+        for c in range(PASSES):
+            gate_derivative(0, c)
+        for c in range(PASSES):
+            times_grad(0, c)
 
         m_grouped = keep.tile([P, PASSES, M, PACK], BF16, align_bytes=64)
         for c in range(PASSES):
             nc.scalar.copy(out=rows_together(m_grouped[:, c]), in_=rows_apart(m_raw[:, c]))
-        nc.vector.quantize_mx(
-            out=m_codes[:].rearrange("p c i -> p (c i)").bitcast(E4M3_X4),
-            scales=m_scales[:].rearrange("p c i -> p (c i)"),
-            in_=m_grouped[:].rearrange("p c i j -> p (c i j)"),
-        )
 
-        quantise_and_multiply(0)
-        for n in range(1, CHUNKS):
-            products(n)
-            quantise_and_multiply(n)
+        for n in range(CHUNKS):
+            acc = [psum.tile([M_TILE, N_TILE], F32, name="acc%d" % t) for t in range(M_TILES)]
+            for c in range(PASSES):
+                times_act(n, c)
+                if n + 1 < CHUNKS:
+                    gate_derivative(n + 1, c)
+                if (n, c) == (0, 0):
+                    nc.vector.quantize_mx(
+                        out=m_codes[:].rearrange("p c i -> p (c i)").bitcast(E4M3_X4),
+                        scales=m_scales[:].rearrange("p c i -> p (c i)"),
+                        in_=m_grouped[:].rearrange("p c i j -> p (c i j)"),
+                    )
+                quantise_and_multiply(n, c, acc)
+            if n + 1 < CHUNKS:
+                for c in range(PASSES):
+                    times_grad(n + 1, c)
+            store(n, acc)

@@ -8,6 +8,7 @@ E4M3_X4 = mybir.dt.float8_e4m3fn_x4
 E5M2_X4 = mybir.dt.float8_e5m2_x4
 MULT = mybir.AluOpType.mult
 SUBTRACT = mybir.AluOpType.subtract
+SQUARE = mybir.ActivationFunctionType.Square
 
 P = 128
 PACK = 4
@@ -20,7 +21,10 @@ M_TILE = P
 M_TILES = M // M_TILE
 N_TILE = 512
 CHUNKS = MD // N_TILE
+UNITS = CHUNKS * PASSES
 RUN = 4
+SQUARES_AHEAD = 3
+M_AFTER_UNIT = 3
 
 FLOPS = 2 * TOKENS * M * MD
 BYTES = TOKENS * M * 2 + TOKENS * MD * (2 + 2 + 4) + M * MD * 4
@@ -43,58 +47,60 @@ def tile_edrncell_pa_v_kernel(
     act_rows = a_t.rearrange("(c p j) w -> c p j w", p=P, j=PACK)
 
     with (
-        tc.tile_pool(name="inputs", bufs=CHUNKS * PASSES) as inputs,
+        tc.tile_pool(name="inputs", bufs=UNITS) as inputs,
         tc.tile_pool(name="keep", bufs=1) as keep,
         tc.tile_pool(name="stage", bufs=4) as stage,
+        tc.tile_pool(name="results", bufs=CHUNKS * M_TILES) as results,
         tc.psum_pool(name="psum", bufs=2) as psum,
         tc.manual_schedule(),
     ):
         gate, grad, act, dz = {}, {}, {}, {}
 
-        def load_chunk(n):
+        def load_unit(u):
+            n, c = divmod(u, PASSES)
             cols = slice(n * N_TILE, (n + 1) * N_TILE)
-            for c in range(PASSES):
-                gate_tile = inputs.tile([P, PACK, N_TILE], F32)
-                nc.sync.dma_start(out=gate_tile[:], in_=gate_rows[c, :, :, cols])
-                gate[n, c] = gate_tile
-            for c in range(PASSES):
-                grad_tile = inputs.tile([P, PACK, N_TILE], BF16)
-                nc.sync.dma_start(out=grad_tile[:], in_=grad_rows[c, :, :, cols])
-                grad[n, c] = grad_tile
-            if n == 0:
-                nc.sync.dma_start(out=m_raw[:], in_=m_t.rearrange("(c p j) i -> p c j i", p=P, j=PACK))
-            for c in range(PASSES):
-                act_tile = inputs.tile([P, PACK, N_TILE], BF16)
-                nc.sync.dma_start(out=act_tile[:], in_=act_rows[c, :, :, cols])
-                act[n, c] = act_tile
+            gate_tile = inputs.tile([P, PACK, N_TILE], F32)
+            nc.sync.dma_start(out=gate_tile[:], in_=gate_rows[c, :, :, cols])
+            gate[u] = gate_tile
+            grad_tile = inputs.tile([P, PACK, N_TILE], BF16)
+            nc.sync.dma_start(out=grad_tile[:], in_=grad_rows[c, :, :, cols])
+            grad[u] = grad_tile
+            act_tile = inputs.tile([P, PACK, N_TILE], BF16)
+            nc.sync.dma_start(out=act_tile[:], in_=act_rows[c, :, :, cols])
+            act[u] = act_tile
 
-        def gate_derivative(n, c):
-            g = gate[n, c]
-            nc.vector.scalar_tensor_tensor(out=g[:], in0=g[:], scalar=1.0, in1=g[:], op0=SUBTRACT, op1=MULT)
+        def square(u):
+            g = gate[u]
+            nc.scalar.activation(out=g[:], in_=g[:], func=SQUARE, bias=-0.5, scale=1.0)
 
-        def times_grad(n, c):
-            g = gate[n, c]
+        def times_grad(u):
+            g = gate[u]
             nc.vector.scalar_tensor_tensor(
-                out=g[:], in0=g[:], scalar=-1.0, in1=grad[n, c][:], op0=MULT, op1=MULT
+                out=g[:], in0=g[:], scalar=0.25, in1=grad[u][:], op0=SUBTRACT, op1=MULT
             )
 
-        def times_act(n, c):
+        def times_act(u):
             dz_tile = stage.tile([P, N_TILE, PACK], BF16, align_bytes=64)
             nc.vector.tensor_tensor(
                 out=rows_together(dz_tile[:]),
-                in0=rows_apart(gate[n, c][:]),
-                in1=rows_apart(act[n, c][:]),
+                in0=rows_apart(gate[u][:]),
+                in1=rows_apart(act[u][:]),
                 op=MULT,
             )
-            dz[n, c] = dz_tile
+            dz[u] = dz_tile
 
-        def quantise_and_multiply(n, c, acc):
+        def quantise(u):
+            n, c = divmod(u, PASSES)
             cols = slice(n * N_TILE, (n + 1) * N_TILE)
             nc.vector.quantize_mx(
                 out=dz_codes[:, c, cols].bitcast(E5M2_X4),
                 scales=dz_scales[:, c, cols],
-                in_=dz[n, c][:].rearrange("p w j -> p (w j)"),
+                in_=dz[u][:].rearrange("p w j -> p (w j)"),
             )
+
+        def multiply(u, acc):
+            n, c = divmod(u, PASSES)
+            cols = slice(n * N_TILE, (n + 1) * N_TILE)
             for t in range(M_TILES):
                 m_cols = slice(t * M_TILE, (t + 1) * M_TILE)
                 nc.tensor.matmul_mx(
@@ -110,45 +116,55 @@ def tile_edrncell_pa_v_kernel(
         def store(n, acc):
             cols = slice(n * N_TILE, (n + 1) * N_TILE)
             for t in range(M_TILES):
-                result = stage.tile([M_TILE, N_TILE], F32)
+                result = results.tile([M_TILE, N_TILE], F32)
                 if n == CHUNKS - 1 and t % 2 == 1:
-                    nc.vector.tensor_copy(out=result[:], in_=acc[t][:])
+                    nc.vector.tensor_scalar_mul(out=result[:], in0=acc[t][:], scalar1=-1.0)
                 else:
-                    nc.scalar.copy(out=result[:], in_=acc[t][:])
+                    nc.scalar.mul(out=result[:], in_=acc[t][:], mul=-1.0)
                 nc.sync.dma_start(out=out[t * M_TILE : (t + 1) * M_TILE, cols], in_=result[:])
 
         m_raw = keep.tile([P, PASSES, PACK, M], BF16)
-        for n in range(CHUNKS):
-            load_chunk(n)
+        for u in range(UNITS):
+            load_unit(u)
+            if u == M_AFTER_UNIT:
+                nc.sync.dma_start(out=m_raw[:], in_=m_t.rearrange("(c p j) i -> p c j i", p=P, j=PACK))
 
         m_codes = keep.tile([P, PASSES, M], U32, align_bytes=64)
         m_scales = keep.tile([P, PASSES, M], U8, align_bytes=64)
         dz_codes = keep.tile([P, PASSES, MD], U32, align_bytes=64)
         dz_scales = keep.tile([P, PASSES, MD], U8, align_bytes=64)
-
-        for c in range(PASSES):
-            gate_derivative(0, c)
-        for c in range(PASSES):
-            times_grad(0, c)
-
         m_grouped = keep.tile([P, PASSES, M, PACK], BF16, align_bytes=64)
-        for c in range(PASSES):
-            nc.scalar.copy(out=rows_together(m_grouped[:, c]), in_=rows_apart(m_raw[:, c]))
 
-        for n in range(CHUNKS):
-            acc = [psum.tile([M_TILE, N_TILE], F32, name="acc%d" % t) for t in range(M_TILES)]
-            for c in range(PASSES):
-                times_act(n, c)
-                if n + 1 < CHUNKS:
-                    gate_derivative(n + 1, c)
-                if (n, c) == (0, 0):
-                    nc.vector.quantize_mx(
-                        out=m_codes[:].rearrange("p c i -> p (c i)").bitcast(E4M3_X4),
-                        scales=m_scales[:].rearrange("p c i -> p (c i)"),
-                        in_=m_grouped[:].rearrange("p c i j -> p (c i j)"),
-                    )
-                quantise_and_multiply(n, c, acc)
-            if n + 1 < CHUNKS:
-                for c in range(PASSES):
-                    times_grad(n + 1, c)
-            store(n, acc)
+        for u in range(SQUARES_AHEAD):
+            square(u)
+        times_grad(0)
+
+        acc = None
+        waiting = []
+        for u in range(UNITS):
+            times_act(u)
+            if u + 1 < UNITS:
+                times_grad(u + 1)
+            if u + SQUARES_AHEAD == M_AFTER_UNIT + 1:
+                nc.scalar.copy(out=rows_together(m_grouped[:, 0]), in_=rows_apart(m_raw[:, 0]))
+            if u + SQUARES_AHEAD < UNITS:
+                square(u + SQUARES_AHEAD)
+            if u + SQUARES_AHEAD == M_AFTER_UNIT + 1:
+                nc.scalar.copy(out=rows_together(m_grouped[:, 1]), in_=rows_apart(m_raw[:, 1]))
+            quantise(u)
+            waiting.append(u)
+            if u == M_AFTER_UNIT:
+                nc.vector.quantize_mx(
+                    out=m_codes[:].rearrange("p c i -> p (c i)").bitcast(E4M3_X4),
+                    scales=m_scales[:].rearrange("p c i -> p (c i)"),
+                    in_=m_grouped[:].rearrange("p c i j -> p (c i j)"),
+                )
+            if u >= M_AFTER_UNIT:
+                for v in waiting:
+                    n, c = divmod(v, PASSES)
+                    if c == 0:
+                        acc = [psum.tile([M_TILE, N_TILE], F32, name="acc%d" % t) for t in range(M_TILES)]
+                    multiply(v, acc)
+                    if c == PASSES - 1:
+                        store(n, acc)
+                waiting.clear()

@@ -21,10 +21,11 @@ M_TILE = P
 M_TILES = M // M_TILE
 N_TILE = 512
 CHUNKS = MD // N_TILE
-UNITS = CHUNKS * PASSES
 RUN = 4
-SQUARES_AHEAD = 3
-M_AFTER_UNIT = 3
+GROUPS = [(0, 2, 0), (0, 2, 1), (2, 2, 0), (2, 2, 1)]
+SQUARES_AHEAD = 2
+M_AFTER_GROUP = 1
+STORES = [(0, 2), (2, 1), (3, 1)]
 
 FLOPS = 2 * TOKENS * M * MD
 BYTES = TOKENS * M * 2 + TOKENS * MD * (2 + 2 + 4) + M * MD * 4
@@ -45,88 +46,96 @@ def tile_edrncell_pa_v_kernel(
     gate_rows = G_fg.rearrange("(c p j) w -> c p j w", p=P, j=PACK)
     grad_rows = grad_out.rearrange("(c p j) w -> c p j w", p=P, j=PACK)
     act_rows = a_t.rearrange("(c p j) w -> c p j w", p=P, j=PACK)
+    last_group = len(GROUPS) - 1
 
     with (
-        tc.tile_pool(name="inputs", bufs=UNITS) as inputs,
         tc.tile_pool(name="keep", bufs=1) as keep,
         tc.tile_pool(name="stage", bufs=4) as stage,
-        tc.tile_pool(name="results", bufs=CHUNKS * M_TILES) as results,
         tc.psum_pool(name="psum", bufs=2) as psum,
         tc.manual_schedule(),
     ):
-        gate, grad, act, dz = {}, {}, {}, {}
+        gate, grad, act, dz, acc, result = {}, {}, {}, {}, {}, {}
 
-        def load_unit(u):
-            n, c = divmod(u, PASSES)
-            cols = slice(n * N_TILE, (n + 1) * N_TILE)
-            gate_tile = inputs.tile([P, PACK, N_TILE], F32)
-            nc.sync.dma_start(out=gate_tile[:], in_=gate_rows[c, :, :, cols])
-            gate[u] = gate_tile
-            grad_tile = inputs.tile([P, PACK, N_TILE], BF16)
-            nc.sync.dma_start(out=grad_tile[:], in_=grad_rows[c, :, :, cols])
-            grad[u] = grad_tile
-            act_tile = inputs.tile([P, PACK, N_TILE], BF16)
-            nc.sync.dma_start(out=act_tile[:], in_=act_rows[c, :, :, cols])
-            act[u] = act_tile
+        def load_group(g):
+            first, count, c = GROUPS[g]
+            cols = slice(first * N_TILE, (first + count) * N_TILE)
+            gate[g] = keep.tile([P, PACK, count * N_TILE], F32, name="gate%d" % g)
+            grad[g] = keep.tile([P, PACK, count * N_TILE], BF16, name="grad%d" % g)
+            for j in range(PACK):
+                nc.sync.dma_start(out=gate[g][:, j, :], in_=gate_rows[c, :, j, cols])
+                nc.sync.dma_start(out=grad[g][:, j, :], in_=grad_rows[c, :, j, cols])
+            for n in range(first, first + count):
+                act[n, c] = keep.tile([P, PACK, N_TILE], BF16, name="act%d_%d" % (n, c))
+                nc.sync.dma_start(out=act[n, c][:], in_=act_rows[c, :, :, n * N_TILE : (n + 1) * N_TILE])
 
-        def square(u):
-            g = gate[u]
-            nc.scalar.activation(out=g[:], in_=g[:], func=SQUARE, bias=-0.5, scale=1.0)
+        def square(g, j):
+            nc.scalar.activation(out=gate[g][:, j, :], in_=gate[g][:, j, :], func=SQUARE, bias=-0.5, scale=1.0)
 
-        def times_grad(u):
-            g = gate[u]
+        def times_grad(g, j):
             nc.vector.scalar_tensor_tensor(
-                out=g[:], in0=g[:], scalar=0.25, in1=grad[u][:], op0=SUBTRACT, op1=MULT
+                out=gate[g][:, j, :], in0=gate[g][:, j, :], scalar=0.25, in1=grad[g][:, j, :], op0=SUBTRACT, op1=MULT
             )
 
-        def times_act(u):
+        def times_act(g, n):
+            first, count, c = GROUPS[g]
             dz_tile = stage.tile([P, N_TILE, PACK], BF16, align_bytes=64)
             nc.vector.tensor_tensor(
                 out=rows_together(dz_tile[:]),
-                in0=rows_apart(gate[u][:]),
-                in1=rows_apart(act[u][:]),
+                in0=rows_apart(gate[g][:, :, (n - first) * N_TILE : (n - first + 1) * N_TILE]),
+                in1=rows_apart(act[n, c][:]),
                 op=MULT,
             )
-            dz[u] = dz_tile
+            dz[n, c] = dz_tile
 
-        def quantise(u):
-            n, c = divmod(u, PASSES)
+        def quantise(n, c):
             cols = slice(n * N_TILE, (n + 1) * N_TILE)
             nc.vector.quantize_mx(
                 out=dz_codes[:, c, cols].bitcast(E5M2_X4),
                 scales=dz_scales[:, c, cols],
-                in_=dz[u][:].rearrange("p w j -> p (w j)"),
+                in_=dz[n, c][:].rearrange("p w j -> p (w j)"),
             )
 
-        def multiply(u, acc):
-            n, c = divmod(u, PASSES)
+        started = set()
+
+        def multiply(n, c):
             cols = slice(n * N_TILE, (n + 1) * N_TILE)
+            if n not in started:
+                acc[n] = [psum.tile([M_TILE, N_TILE], F32, name="acc%d" % t) for t in range(M_TILES)]
             for t in range(M_TILES):
                 m_cols = slice(t * M_TILE, (t + 1) * M_TILE)
                 nc.tensor.matmul_mx(
-                    out=acc[t][:],
+                    out=acc[n][t][:],
                     lhsT=m_codes[:, c, m_cols].bitcast(E4M3_X4),
                     lhsT_scale=m_scales[:, c, m_cols],
                     rhs=dz_codes[:, c, cols].bitcast(E5M2_X4),
                     rhs_scale=dz_scales[:, c, cols],
-                    start=(c == 0),
-                    stop=(c == PASSES - 1),
+                    start=(n not in started),
+                    stop=(n in started),
                 )
+            if n in started:
+                store(n)
+            started.add(n)
 
-        def store(n, acc):
-            cols = slice(n * N_TILE, (n + 1) * N_TILE)
+        def store(n):
+            first, count = [s for s in STORES if s[0] <= n < s[0] + s[1]][0]
             for t in range(M_TILES):
-                result = results.tile([M_TILE, N_TILE], F32)
+                if n == first:
+                    result[first, t] = keep.tile([M_TILE, count * N_TILE], F32, name="result%d_%d" % (first, t))
+                part = result[first, t][:, (n - first) * N_TILE : (n - first + 1) * N_TILE]
                 if n == CHUNKS - 1 and t % 2 == 1:
-                    nc.vector.tensor_scalar_mul(out=result[:], in0=acc[t][:], scalar1=-1.0)
+                    nc.vector.tensor_scalar_mul(out=part, in0=acc[n][t][:], scalar1=-1.0)
                 else:
-                    nc.scalar.mul(out=result[:], in_=acc[t][:], mul=-1.0)
-                nc.sync.dma_start(out=out[t * M_TILE : (t + 1) * M_TILE, cols], in_=result[:])
+                    nc.scalar.mul(out=part, in_=acc[n][t][:], mul=-1.0)
+                if n == first + count - 1:
+                    nc.sync.dma_start(
+                        out=out[t * M_TILE : (t + 1) * M_TILE, first * N_TILE : (first + count) * N_TILE],
+                        in_=result[first, t][:],
+                    )
 
         m_raw = keep.tile([P, PASSES, PACK, M], BF16)
-        for u in range(UNITS):
-            load_unit(u)
-            if u == M_AFTER_UNIT:
+        for g in range(len(GROUPS)):
+            load_group(g)
+            if g == M_AFTER_GROUP:
                 nc.sync.dma_start(out=m_raw[:], in_=m_t.rearrange("(c p j) i -> p c j i", p=P, j=PACK))
 
         m_codes = keep.tile([P, PASSES, M], U32, align_bytes=64)
@@ -135,36 +144,50 @@ def tile_edrncell_pa_v_kernel(
         dz_scales = keep.tile([P, PASSES, MD], U8, align_bytes=64)
         m_grouped = keep.tile([P, PASSES, M, PACK], BF16, align_bytes=64)
 
-        for u in range(SQUARES_AHEAD):
-            square(u)
-        times_grad(0)
+        def regroup_m(piece):
+            c, half = divmod(piece, 2)
+            cols = slice(half * (M // 2), (half + 1) * (M // 2))
+            nc.scalar.copy(out=rows_together(m_grouped[:, c, cols, :]), in_=rows_apart(m_raw[:, c, :, cols]))
 
-        acc = None
+        for g in range(SQUARES_AHEAD):
+            for j in range(PACK):
+                square(g, j)
+        for j in range(PACK):
+            times_grad(0, j)
+
         waiting = []
-        for u in range(UNITS):
-            times_act(u)
-            if u + 1 < UNITS:
-                times_grad(u + 1)
-            if u + SQUARES_AHEAD == M_AFTER_UNIT + 1:
-                nc.scalar.copy(out=rows_together(m_grouped[:, 0]), in_=rows_apart(m_raw[:, 0]))
-            if u + SQUARES_AHEAD < UNITS:
-                square(u + SQUARES_AHEAD)
-            if u + SQUARES_AHEAD == M_AFTER_UNIT + 1:
-                nc.scalar.copy(out=rows_together(m_grouped[:, 1]), in_=rows_apart(m_raw[:, 1]))
-            quantise(u)
-            waiting.append(u)
-            if u == M_AFTER_UNIT:
+        for g in range(len(GROUPS)):
+            first, count, c = GROUPS[g]
+            chunks = list(range(first, first + count))
+            spacer = 0
+            if g == last_group:
+                for n in chunks:
+                    times_act(g, n)
+                    quantise(n, c)
+                    multiply(n, c)
+                continue
+            for n in chunks:
+                times_act(g, n)
+            if count == 1:
+                times_grad(g + 1, 0)
+                spacer = 1
+            for n in chunks:
+                quantise(n, c)
+                waiting.append((n, c))
+            if g + SQUARES_AHEAD <= last_group:
+                for j in range(PACK):
+                    if g + SQUARES_AHEAD == M_AFTER_GROUP + 1:
+                        regroup_m(j)
+                    square(g + SQUARES_AHEAD, j)
+            for j in range(spacer, PACK):
+                times_grad(g + 1, j)
+            if g == M_AFTER_GROUP:
                 nc.vector.quantize_mx(
                     out=m_codes[:].rearrange("p c i -> p (c i)").bitcast(E4M3_X4),
                     scales=m_scales[:].rearrange("p c i -> p (c i)"),
                     in_=m_grouped[:].rearrange("p c i j -> p (c i j)"),
                 )
-            if u >= M_AFTER_UNIT:
-                for v in waiting:
-                    n, c = divmod(v, PASSES)
-                    if c == 0:
-                        acc = [psum.tile([M_TILE, N_TILE], F32, name="acc%d" % t) for t in range(M_TILES)]
-                    multiply(v, acc)
-                    if c == PASSES - 1:
-                        store(n, acc)
+            if g >= M_AFTER_GROUP:
+                for n, cc in waiting:
+                    multiply(n, cc)
                 waiting.clear()

@@ -23,8 +23,7 @@ N_TILE = 512
 CHUNKS = MD // N_TILE
 RUN = 4
 GROUPS = [(0, 2, 0), (0, 2, 1), (2, 2, 0), (2, 2, 1)]
-SQUARES_AHEAD = 2
-M_AFTER_GROUP = 1
+M_GROUP = 1
 STORES = [(0, 2), (2, 1), (3, 1)]
 
 FLOPS = 2 * TOKENS * M * MD
@@ -64,6 +63,8 @@ def tile_edrncell_pa_v_kernel(
             for j in range(PACK):
                 nc.sync.dma_start(out=gate[g][:, j, :], in_=gate_rows[c, :, j, cols])
                 nc.sync.dma_start(out=grad[g][:, j, :], in_=grad_rows[c, :, j, cols])
+            if g == M_GROUP:
+                nc.sync.dma_start(out=m_raw[:], in_=m_t.rearrange("(c p j) i -> p c j i", p=P, j=PACK))
             for n in range(first, first + count):
                 act[n, c] = keep.tile([P, PACK, N_TILE], BF16, name="act%d_%d" % (n, c))
                 nc.sync.dma_start(out=act[n, c][:], in_=act_rows[c, :, :, n * N_TILE : (n + 1) * N_TILE])
@@ -135,8 +136,6 @@ def tile_edrncell_pa_v_kernel(
         m_raw = keep.tile([P, PASSES, PACK, M], BF16)
         for g in range(len(GROUPS)):
             load_group(g)
-            if g == M_AFTER_GROUP:
-                nc.sync.dma_start(out=m_raw[:], in_=m_t.rearrange("(c p j) i -> p c j i", p=P, j=PACK))
 
         m_codes = keep.tile([P, PASSES, M], U32, align_bytes=64)
         m_scales = keep.tile([P, PASSES, M], U8, align_bytes=64)
@@ -149,17 +148,21 @@ def tile_edrncell_pa_v_kernel(
             cols = slice(half * (M // 2), (half + 1) * (M // 2))
             nc.scalar.copy(out=rows_together(m_grouped[:, c, cols, :]), in_=rows_apart(m_raw[:, c, :, cols]))
 
-        for g in range(SQUARES_AHEAD):
+        def squares(g):
             for j in range(PACK):
                 square(g, j)
-        for j in range(PACK):
-            times_grad(0, j)
 
+        def first_products(g):
+            for j in range(PACK):
+                times_grad(g, j)
+
+        squares(0)
+        first_products(0)
+        squares(1)
         waiting = []
         for g in range(len(GROUPS)):
             first, count, c = GROUPS[g]
             chunks = list(range(first, first + count))
-            spacer = 0
             if g == last_group:
                 for n in chunks:
                     times_act(g, n)
@@ -168,26 +171,25 @@ def tile_edrncell_pa_v_kernel(
                 continue
             for n in chunks:
                 times_act(g, n)
-            if count == 1:
-                times_grad(g + 1, 0)
-                spacer = 1
-            for n in chunks:
-                quantise(n, c)
-                waiting.append((n, c))
-            if g + SQUARES_AHEAD <= last_group:
-                for j in range(PACK):
-                    if g + SQUARES_AHEAD == M_AFTER_GROUP + 1:
-                        regroup_m(j)
-                    square(g + SQUARES_AHEAD, j)
-            for j in range(spacer, PACK):
-                times_grad(g + 1, j)
-            if g == M_AFTER_GROUP:
+            if g == M_GROUP:
                 nc.vector.quantize_mx(
                     out=m_codes[:].rearrange("p c i -> p (c i)").bitcast(E4M3_X4),
                     scales=m_scales[:].rearrange("p c i -> p (c i)"),
                     in_=m_grouped[:].rearrange("p c i j -> p (c i j)"),
                 )
-            if g >= M_AFTER_GROUP:
                 for n, cc in waiting:
                     multiply(n, cc)
                 waiting.clear()
+            for n in chunks:
+                quantise(n, c)
+                waiting.append((n, c))
+            if g >= M_GROUP:
+                for n, cc in waiting:
+                    multiply(n, cc)
+                waiting.clear()
+            if g == M_GROUP - 1:
+                for piece in range(2 * PASSES):
+                    regroup_m(piece)
+            first_products(g + 1)
+            if g + 2 <= last_group:
+                squares(g + 2)

@@ -152,25 +152,34 @@ def tile_edrncell_pa_v_kernel(
             for j in range(PACK):
                 square(g, j)
 
-        def first_products(g):
-            for j in range(PACK):
+        def first_products(g, slots):
+            for j in slots:
                 times_grad(g, j)
 
         squares(0)
-        first_products(0)
+        first_products(0, range(PACK))
         squares(1)
         waiting = []
+        held = []
         for g in range(len(GROUPS)):
             first, count, c = GROUPS[g]
             chunks = list(range(first, first + count))
             if g == last_group:
-                for n in chunks:
+                quantise(*held[0])
+                multiply(*held[0])
+                for i, n in enumerate(chunks):
                     times_act(g, n)
+                    if i + 1 < len(held):
+                        quantise(*held[i + 1])
                     quantise(n, c)
                     multiply(n, c)
+                    if i + 1 < len(held):
+                        multiply(*held[i + 1])
                 continue
             for n in chunks:
                 times_act(g, n)
+            early = 1 if count == 1 else 0
+            first_products(g + 1, range(early))
             if g == M_GROUP:
                 nc.vector.quantize_mx(
                     out=m_codes[:].rearrange("p c i -> p (c i)").bitcast(E4M3_X4),
@@ -180,9 +189,12 @@ def tile_edrncell_pa_v_kernel(
                 for n, cc in waiting:
                     multiply(n, cc)
                 waiting.clear()
-            for n in chunks:
-                quantise(n, c)
-                waiting.append((n, c))
+            if g == last_group - 1:
+                held.extend([(n, c) for n in chunks])
+            else:
+                for n in chunks:
+                    quantise(n, c)
+                    waiting.append((n, c))
             if g >= M_GROUP:
                 for n, cc in waiting:
                     multiply(n, cc)
@@ -190,6 +202,6 @@ def tile_edrncell_pa_v_kernel(
             if g == M_GROUP - 1:
                 for piece in range(2 * PASSES):
                     regroup_m(piece)
-            first_products(g + 1)
+            first_products(g + 1, range(early, PACK))
             if g + 2 <= last_group:
                 squares(g + 2)

@@ -21,7 +21,7 @@ M_TILE = P
 M_TILES = M // M_TILE
 N_TILE = 512
 CHUNKS = MD // N_TILE
-RUN = 4
+RUN = 8
 GROUPS = [(0, 2, 0), (0, 2, 1), (2, 2, 0), (2, 2, 1)]
 M_GROUP = 1
 STORES = [(0, 2), (2, 1), (3, 1)]

@@ -23,7 +23,6 @@ N_TILE = 512
 CHUNKS = MD // N_TILE
 RUN = 8
 GROUPS = [(0, 2, 0), (0, 2, 1), (2, 2, 0), (2, 2, 1)]
-M_GROUP = 1
 STORES = [(0, 2), (2, 1), (3, 1)]
 
 FLOPS = 2 * TOKENS * M * MD
@@ -63,8 +62,6 @@ def tile_edrncell_pa_v_kernel(
             for j in range(PACK):
                 nc.sync.dma_start(out=gate[g][:, j, :], in_=gate_rows[c, :, j, cols])
                 nc.sync.dma_start(out=grad[g][:, j, :], in_=grad_rows[c, :, j, cols])
-            if g == M_GROUP:
-                nc.sync.dma_start(out=m_raw[:], in_=m_t.rearrange("(c p j) i -> p c j i", p=P, j=PACK))
             for n in range(first, first + count):
                 act[n, c] = keep.tile([P, PACK, N_TILE], BF16, name="act%d_%d" % (n, c))
                 nc.sync.dma_start(out=act[n, c][:], in_=act_rows[c, :, :, n * N_TILE : (n + 1) * N_TILE])
@@ -134,6 +131,7 @@ def tile_edrncell_pa_v_kernel(
                     )
 
         m_raw = keep.tile([P, PASSES, PACK, M], BF16)
+        nc.sync.dma_start(out=m_raw[:], in_=m_t.rearrange("(c p j) i -> p c j i", p=P, j=PACK))
         for g in range(len(GROUPS)):
             load_group(g)
 
@@ -143,10 +141,6 @@ def tile_edrncell_pa_v_kernel(
         dz_scales = keep.tile([P, PASSES, MD], U8, align_bytes=64)
         m_grouped = keep.tile([P, PASSES, M, PACK], BF16, align_bytes=64)
 
-        def regroup_m(piece):
-            c, half = divmod(piece, 2)
-            cols = slice(half * (M // 2), (half + 1) * (M // 2))
-            nc.scalar.copy(out=rows_together(m_grouped[:, c, cols, :]), in_=rows_apart(m_raw[:, c, :, cols]))
 
         def squares(g):
             for j in range(PACK):
@@ -156,10 +150,17 @@ def tile_edrncell_pa_v_kernel(
             for j in slots:
                 times_grad(g, j)
 
+        for c in range(PASSES):
+            nc.vector.tensor_copy(out=rows_together(m_grouped[:, c]), in_=rows_apart(m_raw[:, c]))
         squares(0)
-        first_products(0, range(PACK))
+        first_products(0, range(1))
+        nc.vector.quantize_mx(
+            out=m_codes[:].rearrange("p c i -> p (c i)").bitcast(E4M3_X4),
+            scales=m_scales[:].rearrange("p c i -> p (c i)"),
+            in_=m_grouped[:].rearrange("p c i j -> p (c i j)"),
+        )
+        first_products(0, range(1, PACK))
         squares(1)
-        waiting = []
         held = []
         for g in range(len(GROUPS)):
             first, count, c = GROUPS[g]
@@ -178,30 +179,12 @@ def tile_edrncell_pa_v_kernel(
                 continue
             for n in chunks:
                 times_act(g, n)
-            early = 1 if count == 1 else 0
-            first_products(g + 1, range(early))
-            if g == M_GROUP:
-                nc.vector.quantize_mx(
-                    out=m_codes[:].rearrange("p c i -> p (c i)").bitcast(E4M3_X4),
-                    scales=m_scales[:].rearrange("p c i -> p (c i)"),
-                    in_=m_grouped[:].rearrange("p c i j -> p (c i j)"),
-                )
-                for n, cc in waiting:
-                    multiply(n, cc)
-                waiting.clear()
             if g == last_group - 1:
                 held.extend([(n, c) for n in chunks])
             else:
                 for n in chunks:
                     quantise(n, c)
-                    waiting.append((n, c))
-            if g >= M_GROUP:
-                for n, cc in waiting:
-                    multiply(n, cc)
-                waiting.clear()
-            if g == M_GROUP - 1:
-                for piece in range(2 * PASSES):
-                    regroup_m(piece)
-            first_products(g + 1, range(early, PACK))
+                    multiply(n, c)
+            first_products(g + 1, range(PACK))
             if g + 2 <= last_group:
                 squares(g + 2)

@@ -66,13 +66,21 @@ def tile_edrncell_pa_v_kernel(
                 act[n, c] = keep.tile([P, PACK, N_TILE], BF16, name="act%d_%d" % (n, c))
                 nc.sync.dma_start(out=act[n, c][:], in_=act_rows[c, :, :, n * N_TILE : (n + 1) * N_TILE])
 
+        def parts(g, j):
+            count = GROUPS[g][1]
+            if j == PACK - 1:
+                return [slice(h * N_TILE, (h + 1) * N_TILE) for h in range(count)]
+            return [slice(0, count * N_TILE)]
+
         def square(g, j):
-            nc.scalar.activation(out=gate[g][:, j, :], in_=gate[g][:, j, :], func=SQUARE, bias=-0.5, scale=1.0)
+            for w in parts(g, j):
+                nc.scalar.activation(out=gate[g][:, j, w], in_=gate[g][:, j, w], func=SQUARE, bias=-0.5, scale=1.0)
 
         def times_grad(g, j):
-            nc.vector.scalar_tensor_tensor(
-                out=gate[g][:, j, :], in0=gate[g][:, j, :], scalar=0.25, in1=grad[g][:, j, :], op0=SUBTRACT, op1=MULT
-            )
+            for w in parts(g, j):
+                nc.vector.scalar_tensor_tensor(
+                    out=gate[g][:, j, w], in0=gate[g][:, j, w], scalar=0.25, in1=grad[g][:, j, w], op0=SUBTRACT, op1=MULT
+                )
 
         def times_act(g, n):
             first, count, c = GROUPS[g]

@@ -82,24 +82,28 @@ def tile_edrncell_pa_v_kernel(
                     out=gate[g][:, j, w], in0=gate[g][:, j, w], scalar=0.25, in1=grad[g][:, j, w], op0=SUBTRACT, op1=MULT
                 )
 
-        def times_act(g, n):
+        def times_act(g, n, pieces=1):
             first, count, c = GROUPS[g]
             dz_tile = stage.tile([P, N_TILE, PACK], BF16, align_bytes=64)
-            nc.vector.tensor_tensor(
-                out=rows_together(dz_tile[:]),
-                in0=rows_apart(gate[g][:, :, (n - first) * N_TILE : (n - first + 1) * N_TILE]),
-                in1=rows_apart(act[n, c][:]),
-                op=MULT,
-            )
+            width = N_TILE // pieces
+            for i in range(pieces):
+                nc.vector.tensor_tensor(
+                    out=rows_together(dz_tile[:, i * width : (i + 1) * width, :]),
+                    in0=rows_apart(gate[g][:, :, (n - first) * N_TILE + i * width : (n - first) * N_TILE + (i + 1) * width]),
+                    in1=rows_apart(act[n, c][:, :, i * width : (i + 1) * width]),
+                    op=MULT,
+                )
             dz[n, c] = dz_tile
 
-        def quantise(n, c):
-            cols = slice(n * N_TILE, (n + 1) * N_TILE)
-            nc.vector.quantize_mx(
-                out=dz_codes[:, c, cols].bitcast(E5M2_X4),
-                scales=dz_scales[:, c, cols],
-                in_=dz[n, c][:].rearrange("p w j -> p (w j)"),
-            )
+        def quantise(n, c, pieces=1):
+            width = N_TILE // pieces
+            for i in range(pieces):
+                cols = slice(n * N_TILE + i * width, n * N_TILE + (i + 1) * width)
+                nc.vector.quantize_mx(
+                    out=dz_codes[:, c, cols].bitcast(E5M2_X4),
+                    scales=dz_scales[:, c, cols],
+                    in_=dz[n, c][:, i * width : (i + 1) * width, :].rearrange("p w j -> p (w j)"),
+                )
 
         started = set()
 
@@ -177,10 +181,11 @@ def tile_edrncell_pa_v_kernel(
                 quantise(*held[0])
                 multiply(*held[0])
                 for i, n in enumerate(chunks):
-                    times_act(g, n)
+                    pieces = 2 if n == chunks[-1] else 1
+                    times_act(g, n, pieces)
                     if i + 1 < len(held):
                         quantise(*held[i + 1])
-                    quantise(n, c)
+                    quantise(n, c, pieces)
                     multiply(n, c)
                     if i + 1 < len(held):
                         multiply(*held[i + 1])

@@ -143,9 +143,12 @@ def tile_edrncell_pa_v_kernel(
                     )
 
         m_raw = keep.tile([P, PASSES, PACK, M], BF16)
-        nc.sync.dma_start(out=m_raw[:], in_=m_t.rearrange("(c p j) i -> p c j i", p=P, j=PACK))
+        m_rows = m_t.rearrange("(c p j) i -> c p j i", p=P, j=PACK)
+        nc.sync.dma_start(out=m_raw[:, 0], in_=m_rows[0])
         for g in range(len(GROUPS)):
             load_group(g)
+            if g == 0:
+                nc.sync.dma_start(out=m_raw[:, 1], in_=m_rows[1])
 
         m_codes = keep.tile([P, PASSES, M], U32, align_bytes=64)
         m_scales = keep.tile([P, PASSES, M], U8, align_bytes=64)
@@ -162,16 +165,20 @@ def tile_edrncell_pa_v_kernel(
             for j in slots:
                 times_grad(g, j)
 
-        for c in range(PASSES):
-            nc.vector.tensor_copy(out=rows_together(m_grouped[:, c]), in_=rows_apart(m_raw[:, c]))
+        def quantise_m(c):
+            nc.vector.quantize_mx(
+                out=m_codes[:, c, :].bitcast(E4M3_X4),
+                scales=m_scales[:, c, :],
+                in_=m_grouped[:, c].rearrange("p i j -> p (i j)"),
+            )
+
+        nc.vector.tensor_copy(out=rows_together(m_grouped[:, 0]), in_=rows_apart(m_raw[:, 0]))
         squares(0)
-        first_products(0, range(1))
-        nc.vector.quantize_mx(
-            out=m_codes[:].rearrange("p c i -> p (c i)").bitcast(E4M3_X4),
-            scales=m_scales[:].rearrange("p c i -> p (c i)"),
-            in_=m_grouped[:].rearrange("p c i j -> p (c i j)"),
-        )
-        first_products(0, range(1, PACK))
+        quantise_m(0)
+        first_products(0, range(PACK))
+        for h in range(2):
+            half = slice(h * M // 2, (h + 1) * M // 2)
+            nc.scalar.copy(out=rows_together(m_grouped[:, 1, half, :]), in_=rows_apart(m_raw[:, 1, :, half]))
         squares(1)
         held = []
         for g in range(len(GROUPS)):
@@ -198,6 +205,9 @@ def tile_edrncell_pa_v_kernel(
                 for n in chunks:
                     quantise(n, c)
                     multiply(n, c)
-            first_products(g + 1, range(PACK))
+            first_products(g + 1, range(PACK - 1))
+            if g == 0:
+                quantise_m(1)
+            first_products(g + 1, range(PACK - 1, PACK))
             if g + 2 <= last_group:
                 squares(g + 2)

@@ -131,6 +131,15 @@ def tile_edrncell_pa_v_kernel(
             for t in range(M_TILES):
                 if n == first:
                     result[first, t] = keep.tile([M_TILE, count * N_TILE], F32, name="result%d_%d" % (first, t))
+                if n == CHUNKS - 1 and t == 0:
+                    for h in range(2):
+                        w = slice(h * N_TILE // 2, (h + 1) * N_TILE // 2)
+                        nc.scalar.mul(out=result[first, t][:, w], in_=acc[n][t][:, w], mul=-1.0)
+                        nc.sync.dma_start(
+                            out=out[t * M_TILE : (t + 1) * M_TILE, n * N_TILE + h * N_TILE // 2 : n * N_TILE + (h + 1) * N_TILE // 2],
+                            in_=result[first, t][:, w],
+                        )
+                    continue
                 part = result[first, t][:, (n - first) * N_TILE : (n - first + 1) * N_TILE]
                 if n == CHUNKS - 1 and t % 2 == 1:
                     nc.vector.tensor_scalar_mul(out=part, in0=acc[n][t][:], scalar1=-1.0)

import concourse.mybir as mybir

F32 = mybir.dt.float32
BF16 = mybir.dt.bfloat16
U32 = mybir.dt.uint32
U8 = mybir.dt.uint8
E4M3_X4 = mybir.dt.float8_e4m3fn_x4
E5M2_X4 = mybir.dt.float8_e5m2_x4
MULT = mybir.AluOpType.mult
SUBTRACT = mybir.AluOpType.subtract
SQUARE = mybir.ActivationFunctionType.Square

P = 128
PACK = 4
K_PASS = P * PACK
TOKENS = 1024
M = 512
MD = 2048
PASSES = TOKENS // K_PASS
M_TILE = P
M_TILES = M // M_TILE
N_TILE = 512
CHUNKS = MD // N_TILE
RUN = 8
GROUPS = [(0, 2, 0), (0, 2, 1), (2, 2, 0), (2, 2, 1)]
STORES = [(0, 2), (2, 1), (3, 1)]

FLOPS = 2 * TOKENS * M * MD
BYTES = TOKENS * M * 2 + TOKENS * MD * (2 + 2 + 4) + M * MD * 4


def rows_apart(tile_ap):
    return tile_ap.rearrange("p j (q i) -> p q j i", i=RUN)


def rows_together(tile_ap):
    return tile_ap.rearrange("p (q i) j -> p q j i", i=RUN)


def tile_edrncell_pa_v_kernel(
    tc, x_t, m_t, a_t, A_fg, A_in, A_th, A_pt_blk, B_fg, B_in, B_th, b_fg, b_in, b_th, G_fg, grad_out, out
):
    nc = tc.nc
    gate_rows = G_fg.rearrange("(c p j) w -> c p j w", p=P, j=PACK)
    grad_rows = grad_out.rearrange("(c p j) w -> c p j w", p=P, j=PACK)
    act_rows = a_t.rearrange("(c p j) w -> c p j w", p=P, j=PACK)
    last_group = len(GROUPS) - 1

    with (
        tc.tile_pool(name="keep", bufs=1) as keep,
        tc.tile_pool(name="stage", bufs=4) as stage,
        tc.psum_pool(name="psum", bufs=2) as psum,
        tc.manual_schedule(),
    ):
        gate, grad, act, dz, acc, result = {}, {}, {}, {}, {}, {}

        def load_group(g):
            first, count, c = GROUPS[g]
            cols = slice(first * N_TILE, (first + count) * N_TILE)
            gate[g] = keep.tile([P, PACK, count * N_TILE], F32, name="gate%d" % g)
            grad[g] = keep.tile([P, PACK, count * N_TILE], BF16, name="grad%d" % g)
            for j in range(PACK):
                nc.sync.dma_start(out=gate[g][:, j, :], in_=gate_rows[c, :, j, cols])
                nc.sync.dma_start(out=grad[g][:, j, :], in_=grad_rows[c, :, j, cols])
            for n in range(first, first + count):
                act[n, c] = keep.tile([P, PACK, N_TILE], BF16, name="act%d_%d" % (n, c))
                nc.sync.dma_start(out=act[n, c][:], in_=act_rows[c, :, :, n * N_TILE : (n + 1) * N_TILE])

        def parts(g, j):
            count = GROUPS[g][1]
            if j == PACK - 1:
                return [slice(h * N_TILE, (h + 1) * N_TILE) for h in range(count)]
            return [slice(0, count * N_TILE)]

        def square(g, j):
            for w in parts(g, j):
                nc.scalar.activation(out=gate[g][:, j, w], in_=gate[g][:, j, w], func=SQUARE, bias=-0.5, scale=1.0)

        def times_grad(g, j):
            for w in parts(g, j):
                nc.vector.scalar_tensor_tensor(
                    out=gate[g][:, j, w], in0=gate[g][:, j, w], scalar=0.25, in1=grad[g][:, j, w], op0=SUBTRACT, op1=MULT
                )

        def times_act(g, n, pieces=1):
            first, count, c = GROUPS[g]
            dz_tile = stage.tile([P, N_TILE, PACK], BF16, align_bytes=64)
            width = N_TILE // pieces
            for i in range(pieces):
                nc.vector.tensor_tensor(
                    out=rows_together(dz_tile[:, i * width : (i + 1) * width, :]),
                    in0=rows_apart(gate[g][:, :, (n - first) * N_TILE + i * width : (n - first) * N_TILE + (i + 1) * width]),
                    in1=rows_apart(act[n, c][:, :, i * width : (i + 1) * width]),
                    op=MULT,
                )
            dz[n, c] = dz_tile

        def quantise(n, c, pieces=1):
            width = N_TILE // pieces
            for i in range(pieces):
                cols = slice(n * N_TILE + i * width, n * N_TILE + (i + 1) * width)
                nc.vector.quantize_mx(
                    out=dz_codes[:, c, cols].bitcast(E5M2_X4),
                    scales=dz_scales[:, c, cols],
                    in_=dz[n, c][:, i * width : (i + 1) * width, :].rearrange("p w j -> p (w j)"),
                )

        started = set()

        def multiply(n, c):
            cols = slice(n * N_TILE, (n + 1) * N_TILE)
            if n not in started:
                acc[n] = [psum.tile([M_TILE, N_TILE], F32, name="acc%d" % t) for t in range(M_TILES)]
            for t in range(M_TILES):
                m_cols = slice(t * M_TILE, (t + 1) * M_TILE)
                nc.tensor.matmul_mx(
                    out=acc[n][t][:],
                    lhsT=m_codes[:, c, m_cols].bitcast(E4M3_X4),
                    lhsT_scale=m_scales[:, c, m_cols],
                    rhs=dz_codes[:, c, cols].bitcast(E5M2_X4),
                    rhs_scale=dz_scales[:, c, cols],
                    start=(n not in started),
                    stop=(n in started),
                )
            if n in started:
                store(n)
            started.add(n)

        def store(n):
            first, count = [s for s in STORES if s[0] <= n < s[0] + s[1]][0]
            for t in range(M_TILES):
                if n == first:
                    result[first, t] = keep.tile([M_TILE, count * N_TILE], F32, name="result%d_%d" % (first, t))
                if n == CHUNKS - 1 and t == 0:
                    for h in range(2):
                        w = slice(h * N_TILE // 2, (h + 1) * N_TILE // 2)
                        nc.scalar.mul(out=result[first, t][:, w], in_=acc[n][t][:, w], mul=-1.0)
                        nc.sync.dma_start(
                            out=out[t * M_TILE : (t + 1) * M_TILE, n * N_TILE + h * N_TILE // 2 : n * N_TILE + (h + 1) * N_TILE // 2],
                            in_=result[first, t][:, w],
                        )
                    continue
                part = result[first, t][:, (n - first) * N_TILE : (n - first + 1) * N_TILE]
                if n == CHUNKS - 1 and t % 2 == 1:
                    nc.vector.tensor_scalar_mul(out=part, in0=acc[n][t][:], scalar1=-1.0)
                else:
                    nc.scalar.mul(out=part, in_=acc[n][t][:], mul=-1.0)
                if n == first + count - 1:
                    nc.sync.dma_start(
                        out=out[t * M_TILE : (t + 1) * M_TILE, first * N_TILE : (first + count) * N_TILE],
                        in_=result[first, t][:],
                    )

        m_raw = keep.tile([P, PASSES, PACK, M], BF16)
        m_rows = m_t.rearrange("(c p j) i -> c p j i", p=P, j=PACK)
        nc.sync.dma_start(out=m_raw[:, 0], in_=m_rows[0])
        for g in range(len(GROUPS)):
            load_group(g)
            if g == 0:
                nc.sync.dma_start(out=m_raw[:, 1], in_=m_rows[1])

        m_codes = keep.tile([P, PASSES, M], U32, align_bytes=64)
        m_scales = keep.tile([P, PASSES, M], U8, align_bytes=64)
        dz_codes = keep.tile([P, PASSES, MD], U32, align_bytes=64)
        dz_scales = keep.tile([P, PASSES, MD], U8, align_bytes=64)
        m_grouped = keep.tile([P, PASSES, M, PACK], BF16, align_bytes=64)


        def squares(g):
            for j in range(PACK):
                square(g, j)

        def first_products(g, slots):
            for j in slots:
                times_grad(g, j)

        def quantise_m(c):
            nc.vector.quantize_mx(
                out=m_codes[:, c, :].bitcast(E4M3_X4),
                scales=m_scales[:, c, :],
                in_=m_grouped[:, c].rearrange("p i j -> p (i j)"),
            )

        nc.vector.tensor_copy(out=rows_together(m_grouped[:, 0]), in_=rows_apart(m_raw[:, 0]))
        squares(0)
        quantise_m(0)
        first_products(0, range(PACK))
        for h in range(2):
            half = slice(h * M // 2, (h + 1) * M // 2)
            nc.scalar.copy(out=rows_together(m_grouped[:, 1, half, :]), in_=rows_apart(m_raw[:, 1, :, half]))
        squares(1)
        held = []
        for g in range(len(GROUPS)):
            first, count, c = GROUPS[g]
            chunks = list(range(first, first + count))
            if g == last_group:
                quantise(*held[0])
                multiply(*held[0])
                for i, n in enumerate(chunks):
                    pieces = 2 if n == chunks[-1] else 1
                    times_act(g, n, pieces)
                    if i + 1 < len(held):
                        quantise(*held[i + 1])
                    quantise(n, c, pieces)
                    multiply(n, c)
                    if i + 1 < len(held):
                        multiply(*held[i + 1])
                continue
            for n in chunks:
                times_act(g, n)
            if g == last_group - 1:
                held.extend([(n, c) for n in chunks])
            else:
                for n in chunks:
                    quantise(n, c)
                    multiply(n, c)
            first_products(g + 1, range(PACK - 1))
            if g == 0:
                quantise_m(1)
            first_products(g + 1, range(PACK - 1, PACK))
            if g + 2 <= last_group:
                squares(g + 2)
